import numpy as np
import ml_dtypes


def mxq(x, axis, fmt="e4m3"):
    dtype, down = {"e4m3": (ml_dtypes.float8_e4m3fn, 7), "e5m2": (ml_dtypes.float8_e5m2, 14)}[fmt]
    v = np.moveaxis(np.asarray(x, np.float32).astype(ml_dtypes.bfloat16).astype(np.float64), axis, -1)
    blocks = v.reshape(v.shape[:-1] + (-1, 32))
    amax = np.abs(blocks).max(-1, keepdims=True)
    byte = np.maximum(np.where(amax > 0, np.frexp(amax)[1] - 1 + 127, 0) - down, 1)
    scale = np.exp2(byte - 127.0)
    codes = (blocks / scale).astype(np.float32).astype(dtype).astype(np.float64)
    return np.moveaxis((codes * scale).reshape(v.shape), -1, axis)


WIDE = False


def mx_kscale(k):
    if not WIDE:
        return np.ones(k)
    levels = np.array([10, -10, 5, -5, 0])
    a = np.random.permutation(np.resize(levels, k // 512 * 4)).reshape(k // 512, 4)
    idx = np.arange(k)
    return np.exp2(a[idx // 512, idx % 128 // 32])


BF16 = ml_dtypes.bfloat16


def bf(x):
    return np.asarray(x, np.float32).astype(BF16)


def f64(x):
    return np.asarray(x).astype(np.float64)


B, C, C8, H, W, S = 1, 512, 128, 64, 64, 32
T = H * W
S2 = S * S
PH, PW = H // S, W // S


def setup_inputs():
    s = mx_kscale(C)
    return {"x": bf(np.random.standard_normal((B, C, H, W)) * s[None, :, None, None]),
            "Wq": bf(np.random.standard_normal((C8, C)) * 2.0 / np.sqrt(C) / s[None, :]),
            "bq": bf(np.random.standard_normal(C8) * 0.5),
            "Wk": bf(np.random.standard_normal((C8, C)) * 2.0 / np.sqrt(C) / s[None, :]),
            "bk": bf(np.random.standard_normal(C8) * 0.3)}


def reference(x, Wq, bq, Wk, bk):
    xq = mxq(f64(x).reshape(B, C, T), 1, "e4m3")
    qc = (mxq(f64(Wq), 1, "e4m3") @ xq) + f64(bq)[None, :, None]
    kc = (mxq(f64(Wk), 1, "e4m3") @ xq) + f64(bk)[None, :, None]
    q = qc.transpose(0, 2, 1)
    k_pool = kc.reshape(B, C8, S, PH, S, PW).mean(axis=(3, 5)).reshape(B, C8, S2)
    return q, k_pool

@@ -1,0 +1,211 @@
+from contextlib import ExitStack
+
+import concourse.mybir as mybir
+from concourse.masks import make_identity
+
+BF16 = mybir.dt.bfloat16
+F32 = mybir.dt.float32
+U32 = mybir.dt.uint32
+U8 = mybir.dt.uint8
+FP8X4 = mybir.dt.float8_e4m3fn_x4
+ADD = mybir.AluOpType.add
+MULT = mybir.AluOpType.mult
+IDENTITY = mybir.ActivationFunctionType.Identity
+
+P = 128
+PACK = 4
+C = P * PACK
+O = 128
+SIDE = 64
+PIXELS = SIDE * SIDE
+BANK = 512
+
+CHUNK_ROWS = 16
+CHUNK = CHUNK_ROWS * SIDE
+N_CHUNKS = SIDE // CHUNK_ROWS
+PAIRS = CHUNK // 2
+SLICES = PAIRS // P
+POOLED_ROWS = CHUNK_ROWS // 2
+POOLED_SIDE = SIDE // 2
+POOLED = POOLED_ROWS * POOLED_SIDE
+
+VECTOR_PAIRS = PAIRS * 3 // 8
+
+FLOPS = 2 * 2 * O * C * PIXELS
+
+assert SIDE % CHUNK_ROWS == 0 and CHUNK_ROWS % 2 == 0
+assert PAIRS in (256, 512)
+assert VECTOR_PAIRS % 4 == 0
+
+
+def load_weights(nc, const, Wq, Wk):
+    rows = []
+    for i, weight in enumerate((Wq, Wk)):
+        w_rows = const.tile([O, C], BF16, name="w_rows%d" % i)
+        nc.scalar.dma_start(out=w_rows[:], in_=weight)
+        rows.append(w_rows)
+    return rows
+
+
+def load_biases(nc, const, bq, bk):
+    row0 = const.tile([P, 2 * O], BF16)
+    nc.vector.memset(row0[:], 0.0)
+    nc.scalar.dma_start(out=row0[0:1, 0:O], in_=bq.unsqueeze(0))
+    nc.scalar.dma_start(out=row0[0:1, O : 2 * O], in_=bk.unsqueeze(0))
+    ones = const.tile([P, P], BF16)
+    nc.vector.memset(ones[:], 1.0)
+    return row0, ones
+
+
+def quantise_weights(nc, const, setup_psum, rows):
+    identity = const.tile([P, P], F32)
+    make_identity(nc, identity[:])
+
+    flipped = setup_psum.tile([P, 2, 2, O], F32)
+    for i, w_rows in enumerate(rows):
+        words = w_rows[:].bitcast(F32).rearrange("o (p u) -> o u p", u=2)
+        for u in range(2):
+            nc.tensor.transpose(flipped[:, i, u, :], words[:, u, :], identity[:])
+
+    w_grouped = const.tile([P, 2 * O * PACK], BF16, align_bytes=64)
+    nc.vector.tensor_copy(
+        out=w_grouped[:].bitcast(F32).rearrange("p (i o u) -> p i o u", i=2, u=2),
+        in_=flipped[:].rearrange("p i u o -> p i o u"),
+    )
+    w_codes = const.tile([P, 2 * O], U32, align_bytes=64)
+    w_scales = const.tile([P, 2 * O], U8, align_bytes=64)
+    nc.vector.quantize_mx(out=w_codes[:].bitcast(FP8X4), scales=w_scales[:], in_=w_grouped[:])
+    return w_codes, w_scales
+
+
+def spread_biases(nc, const, setup_psum, row0, ones):
+    spread = setup_psum.tile([P, BANK], F32)
+    nc.tensor.matmul(out=spread[:, 0 : 2 * O], lhsT=ones[:], rhs=row0[:], start=True, stop=True)
+    nc.tensor.matmul(
+        out=spread[:, 2 * O : 2 * O + 32],
+        lhsT=row0[:, O : 2 * O],
+        rhs=ones[:, 0:32],
+        start=True,
+        stop=True,
+    )
+    bq_rows = const.tile([P, O], F32)
+    nc.scalar.activation(out=bq_rows[:], in_=spread[:, 0:O], func=IDENTITY)
+    bk_column = const.tile([O, 1], F32)
+    nc.scalar.activation(out=bk_column[:], in_=spread[:, 2 * O : 2 * O + 1], func=IDENTITY)
+    return bq_rows, bk_column
+
+
+def tile_selfattention_pb_kernel(tc, x, Wq, bq, Wk, bk, out_0, out_1):
+    nc = tc.nc
+    x_rows = x[0].rearrange("(p t) h w -> p t (h w)", t=PACK)
+    q_pairs = out_0[0].rearrange("(s p dj) o -> p s (dj o)", p=P, dj=2)
+    k_pool = out_1[0]
+
+    with ExitStack() as ctx:
+        const = ctx.enter_context(tc.tile_pool(name="const", bufs=1))
+        raw_pool = ctx.enter_context(tc.tile_pool(name="raw", bufs=N_CHUNKS))
+        work = ctx.enter_context(tc.tile_pool(name="work", bufs=3))
+        setup_psum = ctx.enter_context(tc.psum_pool(name="setup_psum", bufs=1))
+        q_psum = ctx.enter_context(tc.psum_pool(name="q_psum", bufs=4))
+        k_psum = ctx.enter_context(tc.psum_pool(name="k_psum", bufs=2))
+        ctx.enter_context(tc.manual_schedule())
+
+        raws = []
+        for c in range(N_CHUNKS):
+            raw = raw_pool.tile([P, PACK, CHUNK], BF16)
+            nc.sync.dma_start(out=raw[:], in_=x_rows[:, :, c * CHUNK : (c + 1) * CHUNK])
+            raws.append(raw)
+
+        w_rows = load_weights(nc, const, Wq, Wk)
+        row0, ones = load_biases(nc, const, bq, bk)
+        w_codes, w_scales = quantise_weights(nc, const, setup_psum, w_rows)
+        bq_rows, bk_column = spread_biases(nc, const, setup_psum, row0, ones)
+
+        def regroup(c):
+            grouped = work.tile([P, 2, PAIRS, PACK], BF16, align_bytes=64)
+            source = raws[c][:].rearrange("p t (pair dj) -> p dj pair t", dj=2)
+            nc.vector.tensor_copy(
+                out=grouped[:, :, :VECTOR_PAIRS, :], in_=source[:, :, :VECTOR_PAIRS, :]
+            )
+            nc.scalar.copy(out=grouped[:, :, VECTOR_PAIRS:, :], in_=source[:, :, VECTOR_PAIRS:, :])
+            return grouped
+
+        def quantise(grouped):
+            codes = work.tile([P, CHUNK], U32, align_bytes=64)
+            scales = work.tile([P, CHUNK], U8, align_bytes=64)
+            nc.vector.quantize_mx(
+                out=codes[:].bitcast(FP8X4),
+                scales=scales[:],
+                in_=grouped[:].rearrange("p dj pair t -> p (dj pair t)"),
+            )
+            return codes, scales
+
+        def multiply(codes, scales):
+            q_banks = []
+            for first in range(0, SLICES, 2):
+                q_bank = q_psum.tile([P, 2, 2, O], F32)
+                for s in range(2):
+                    for dj in range(2):
+                        start_col = dj * PAIRS + (first + s) * P
+                        cols = slice(start_col, start_col + P)
+                        nc.tensor.matmul_mx(
+                            out=q_bank[:, s, dj, :],
+                            lhsT=codes[:, cols].bitcast(FP8X4),
+                            lhsT_scale=scales[:, cols],
+                            rhs=w_codes[:, 0:O].bitcast(FP8X4),
+                            rhs_scale=w_scales[:, 0:O],
+                            start=True,
+                            stop=True,
+                        )
+                q_banks.append(q_bank)
+            k_bank = k_psum.tile([O, PAIRS], F32)
+            for dj in range(2):
+                cols = slice(dj * PAIRS, (dj + 1) * PAIRS)
+                nc.tensor.matmul_mx(
+                    out=k_bank[:],
+                    lhsT=w_codes[:, O : 2 * O].bitcast(FP8X4),
+                    lhsT_scale=w_scales[:, O : 2 * O],
+                    rhs=codes[:, cols].bitcast(FP8X4),
+                    rhs_scale=scales[:, cols],
+                    start=(dj == 0),
+                    stop=(dj == 1),
+                )
+            return q_banks, k_bank
+
+        def finish(c, q_banks, k_bank):
+            q_sb = work.tile([P, SLICES, 2 * O], F32)
+            for b, q_bank in enumerate(q_banks):
+                nc.vector.tensor_tensor(
+                    out=q_sb[:, 2 * b : 2 * b + 2, :].rearrange("p s (dj o) -> p (s dj) o", dj=2),
+                    in0=q_bank[:].rearrange("p s dj o -> p (s dj) o"),
+                    in1=bq_rows[:].unsqueeze(1).to_broadcast([P, 4, O]),
+                    op=ADD,
+                )
+            nc.sync.dma_start(out=q_pairs[:, c * SLICES : (c + 1) * SLICES, :], in_=q_sb[:])
+
+            image_rows = k_bank[:].rearrange("o (m di n) -> o di m n", di=2, n=POOLED_SIDE)
+            lower = work.tile([O, POOLED_ROWS, POOLED_SIDE], F32)
+            nc.scalar.activation(
+                out=lower[:], in_=image_rows[:, 1], func=IDENTITY, bias=bk_column[:], scale=0.25
+            )
+            k_sb = work.tile([O, POOLED_ROWS, POOLED_SIDE], F32)
+            nc.vector.scalar_tensor_tensor(
+                out=k_sb[:], in0=image_rows[:, 0], scalar=0.25, in1=lower[:], op0=MULT, op1=ADD
+            )
+            nc.sync.dma_start(
+                out=k_pool[:, c * POOLED : (c + 1) * POOLED],
+                in_=k_sb[:].rearrange("o m n -> o (m n)"),
+            )
+
+        grouped_next = regroup(0)
+        products = None
+        for c in range(N_CHUNKS):
+            grouped = grouped_next
+            if c + 1 < N_CHUNKS:
+                grouped_next = regroup(c + 1)
+            codes, scales = quantise(grouped)
+            earlier = products
+            products = multiply(codes, scales)
+            if earlier is not None:
+                finish(c - 1, earlier[0], earlier[1])
+        finish(N_CHUNKS - 1, products[0], products[1])

@@ -20,7 +20,7 @@ SIDE = 64
 PIXELS = SIDE * SIDE
 BANK = 512
 
-CHUNK_ROWS = 16
+CHUNK_ROWS = 8
 CHUNK = CHUNK_ROWS * SIDE
 N_CHUNKS = SIDE // CHUNK_ROWS
 PAIRS = CHUNK // 2
@@ -29,7 +29,7 @@ POOLED_ROWS = CHUNK_ROWS // 2
 POOLED_SIDE = SIDE // 2
 POOLED = POOLED_ROWS * POOLED_SIDE
 
-VECTOR_PAIRS = PAIRS * 3 // 8
+VECTOR_PAIRS = PAIRS * 5 // 16
 
 FLOPS = 2 * 2 * O * C * PIXELS
 
@@ -42,7 +42,7 @@ def load_weights(nc, const, Wq, Wk):
     rows = []
     for i, weight in enumerate((Wq, Wk)):
         w_rows = const.tile([O, C], BF16, name="w_rows%d" % i)
-        nc.scalar.dma_start(out=w_rows[:], in_=weight)
+        nc.sync.dma_start(out=w_rows[:], in_=weight)
         rows.append(w_rows)
     return rows
 
@@ -50,8 +50,8 @@ def load_weights(nc, const, Wq, Wk):
 def load_biases(nc, const, bq, bk):
     row0 = const.tile([P, 2 * O], BF16)
     nc.vector.memset(row0[:], 0.0)
-    nc.scalar.dma_start(out=row0[0:1, 0:O], in_=bq.unsqueeze(0))
-    nc.scalar.dma_start(out=row0[0:1, O : 2 * O], in_=bk.unsqueeze(0))
+    nc.sync.dma_start(out=row0[0:1, 0:O], in_=bq.unsqueeze(0))
+    nc.sync.dma_start(out=row0[0:1, O : 2 * O], in_=bk.unsqueeze(0))
     ones = const.tile([P, P], BF16)
     nc.vector.memset(ones[:], 1.0)
     return row0, ones
@@ -110,16 +110,16 @@ def tile_selfattention_pb_kernel(tc, x, Wq, bq, Wk, bk, out_0, out_1):
         k_psum = ctx.enter_context(tc.psum_pool(name="k_psum", bufs=2))
         ctx.enter_context(tc.manual_schedule())
 
-        raws = []
-        for c in range(N_CHUNKS):
+        def load_chunk(c):
             raw = raw_pool.tile([P, PACK, CHUNK], BF16)
             nc.sync.dma_start(out=raw[:], in_=x_rows[:, :, c * CHUNK : (c + 1) * CHUNK])
-            raws.append(raw)
+            return raw
 
+        raws = [load_chunk(0)]
         w_rows = load_weights(nc, const, Wq, Wk)
         row0, ones = load_biases(nc, const, bq, bk)
-        w_codes, w_scales = quantise_weights(nc, const, setup_psum, w_rows)
-        bq_rows, bk_column = spread_biases(nc, const, setup_psum, row0, ones)
+        for c in range(1, N_CHUNKS):
+            raws.append(load_chunk(c))
 
         def regroup(c):
             grouped = work.tile([P, 2, PAIRS, PACK], BF16, align_bytes=64)
@@ -198,14 +198,15 @@ def tile_selfattention_pb_kernel(tc, x, Wq, bq, Wk, bk, out_0, out_1):
             )
 
         grouped_next = regroup(0)
+        w_codes, w_scales = quantise_weights(nc, const, setup_psum, w_rows)
+        bq_rows, bk_column = spread_biases(nc, const, setup_psum, row0, ones)
         products = None
         for c in range(N_CHUNKS):
             grouped = grouped_next
             if c + 1 < N_CHUNKS:
                 grouped_next = regroup(c + 1)
+            if products is not None:
+                finish(c - 1, products[0], products[1])
             codes, scales = quantise(grouped)
-            earlier = products
             products = multiply(codes, scales)
-            if earlier is not None:
-                finish(c - 1, earlier[0], earlier[1])
         finish(N_CHUNKS - 1, products[0], products[1])

@@ -123,11 +123,10 @@ def tile_selfattention_pb_kernel(tc, x, Wq, bq, Wk, bk, out_0, out_1):
 
         def regroup(c):
             grouped = work.tile([P, 2, PAIRS, PACK], BF16, align_bytes=64)
-            source = raws[c][:].rearrange("p t (pair dj) -> p dj pair t", dj=2)
-            nc.vector.tensor_copy(
-                out=grouped[:, :, :VECTOR_PAIRS, :], in_=source[:, :, :VECTOR_PAIRS, :]
-            )
-            nc.scalar.copy(out=grouped[:, :, VECTOR_PAIRS:, :], in_=source[:, :, VECTOR_PAIRS:, :])
+            target = grouped[:].rearrange("p dj pair t -> p pair dj t")
+            source = raws[c][:].rearrange("p t (pair dj) -> p pair dj t", dj=2)
+            nc.vector.tensor_copy(out=target[:, :VECTOR_PAIRS], in_=source[:, :VECTOR_PAIRS])
+            nc.scalar.copy(out=target[:, VECTOR_PAIRS:], in_=source[:, VECTOR_PAIRS:])
             return grouped
 
         def quantise(grouped):

@@ -171,7 +171,15 @@ def tile_selfattention_pb_kernel(tc, x, Wq, bq, Wk, bk, out_0, out_1):
                 )
             return q_banks, k_bank
 
-        def finish(c, q_banks, k_bank):
+        def lower_rows(k_bank):
+            image_rows = k_bank[:].rearrange("o (m di n) -> o di m n", di=2, n=POOLED_SIDE)
+            lower = work.tile([O, POOLED_ROWS, POOLED_SIDE], F32)
+            nc.scalar.activation(
+                out=lower[:], in_=image_rows[:, 1], func=IDENTITY, bias=bk_column[:], scale=0.25
+            )
+            return lower
+
+        def finish(c, q_banks, k_bank, lower):
             q_sb = work.tile([P, SLICES, 2 * O], F32)
             for b, q_bank in enumerate(q_banks):
                 nc.vector.tensor_tensor(
@@ -183,10 +191,6 @@ def tile_selfattention_pb_kernel(tc, x, Wq, bq, Wk, bk, out_0, out_1):
             nc.sync.dma_start(out=q_pairs[:, c * SLICES : (c + 1) * SLICES, :], in_=q_sb[:])
 
             image_rows = k_bank[:].rearrange("o (m di n) -> o di m n", di=2, n=POOLED_SIDE)
-            lower = work.tile([O, POOLED_ROWS, POOLED_SIDE], F32)
-            nc.scalar.activation(
-                out=lower[:], in_=image_rows[:, 1], func=IDENTITY, bias=bk_column[:], scale=0.25
-            )
             k_sb = work.tile([O, POOLED_ROWS, POOLED_SIDE], F32)
             nc.vector.scalar_tensor_tensor(
                 out=k_sb[:], in0=image_rows[:, 0], scalar=0.25, in1=lower[:], op0=MULT, op1=ADD
@@ -196,16 +200,18 @@ def tile_selfattention_pb_kernel(tc, x, Wq, bq, Wk, bk, out_0, out_1):
                 in_=k_sb[:].rearrange("o m n -> o (m n)"),
             )
 
-        grouped_next = regroup(0)
+        grouped = regroup(0)
         w_codes, w_scales = quantise_weights(nc, const, setup_psum, w_rows)
         bq_rows, bk_column = spread_biases(nc, const, setup_psum, row0, ones)
-        products = None
+        earlier = None
         for c in range(N_CHUNKS):
-            grouped = grouped_next
-            if c + 1 < N_CHUNKS:
-                grouped_next = regroup(c + 1)
-            if products is not None:
-                finish(c - 1, products[0], products[1])
             codes, scales = quantise(grouped)
-            products = multiply(codes, scales)
-        finish(N_CHUNKS - 1, products[0], products[1])
+            q_banks, k_bank = multiply(codes, scales)
+            if earlier is not None:
+                lower = lower_rows(earlier[1])
+            if c + 1 < N_CHUNKS:
+                grouped = regroup(c + 1)
+            if earlier is not None:
+                finish(c - 1, earlier[0], earlier[1], lower)
+            earlier = (q_banks, k_bank)
+        finish(N_CHUNKS - 1, earlier[0], earlier[1], lower_rows(earlier[1]))

@@ -30,6 +30,7 @@ POOLED_SIDE = SIDE // 2
 POOLED = POOLED_ROWS * POOLED_SIDE
 
 VECTOR_PAIRS = PAIRS * 5 // 16
+VECTOR_RUNS = VECTOR_PAIRS // 2
 
 FLOPS = 2 * 2 * O * C * PIXELS
 
@@ -123,10 +124,10 @@ def tile_selfattention_pb_kernel(tc, x, Wq, bq, Wk, bk, out_0, out_1):
 
         def regroup(c):
             grouped = work.tile([P, 2, PAIRS, PACK], BF16, align_bytes=64)
-            target = grouped[:].rearrange("p dj pair t -> p pair dj t")
-            source = raws[c][:].rearrange("p t (pair dj) -> p pair dj t", dj=2)
-            nc.vector.tensor_copy(out=target[:, :VECTOR_PAIRS], in_=source[:, :VECTOR_PAIRS])
-            nc.scalar.copy(out=target[:, VECTOR_PAIRS:], in_=source[:, VECTOR_PAIRS:])
+            target = grouped[:].rearrange("p dj (run pair) t -> p run t pair dj", pair=2)
+            source = raws[c][:].rearrange("p t (run pair dj) -> p run t pair dj", pair=2, dj=2)
+            nc.vector.tensor_copy(out=target[:, :VECTOR_RUNS], in_=source[:, :VECTOR_RUNS])
+            nc.scalar.copy(out=target[:, VECTOR_RUNS:], in_=source[:, VECTOR_RUNS:])
             return grouped
 
         def quantise(grouped):

@@ -28,14 +28,16 @@ SLICES = PAIRS // P
 POOLED_ROWS = CHUNK_ROWS // 2
 POOLED_SIDE = SIDE // 2
 POOLED = POOLED_ROWS * POOLED_SIDE
+KEY_CHUNKS = BANK // PAIRS
 
 VECTOR_PAIRS = PAIRS * 5 // 16
-VECTOR_RUNS = VECTOR_PAIRS // 2
 
 FLOPS = 2 * 2 * O * C * PIXELS
 
 assert SIDE % CHUNK_ROWS == 0 and CHUNK_ROWS % 2 == 0
 assert PAIRS in (256, 512)
+assert 2 * SLICES * O <= BANK
+assert N_CHUNKS % KEY_CHUNKS == 0
 assert VECTOR_PAIRS % 4 == 0
 
 
@@ -58,10 +60,7 @@ def load_biases(nc, const, bq, bk):
     return row0, ones
 
 
-def quantise_weights(nc, const, setup_psum, rows):
-    identity = const.tile([P, P], F32)
-    make_identity(nc, identity[:])
-
+def quantise_weights(nc, const, setup_psum, rows, identity):
     flipped = setup_psum.tile([P, 2, 2, O], F32)
     for i, w_rows in enumerate(rows):
         words = w_rows[:].bitcast(F32).rearrange("o (p u) -> o u p", u=2)
@@ -116,6 +115,9 @@ def tile_selfattention_pb_kernel(tc, x, Wq, bq, Wk, bk, out_0, out_1):
             nc.sync.dma_start(out=raw[:], in_=x_rows[:, :, c * CHUNK : (c + 1) * CHUNK])
             return raw
 
+        identity = const.tile([P, P], F32)
+        make_identity(nc, identity[:])
+
         raws = [load_chunk(0)]
         w_rows = load_weights(nc, const, Wq, Wk)
         row0, ones = load_biases(nc, const, bq, bk)
@@ -126,8 +128,9 @@ def tile_selfattention_pb_kernel(tc, x, Wq, bq, Wk, bk, out_0, out_1):
             grouped = work.tile([P, 2, PAIRS, PACK], BF16, align_bytes=64)
             target = grouped[:].rearrange("p dj (run pair) t -> p run t pair dj", pair=2)
             source = raws[c][:].rearrange("p t (run pair dj) -> p run t pair dj", pair=2, dj=2)
-            nc.vector.tensor_copy(out=target[:, :VECTOR_RUNS], in_=source[:, :VECTOR_RUNS])
-            nc.scalar.copy(out=target[:, VECTOR_RUNS:], in_=source[:, VECTOR_RUNS:])
+            vector_runs = VECTOR_PAIRS // 2
+            nc.vector.tensor_copy(out=target[:, :vector_runs], in_=source[:, :vector_runs])
+            nc.scalar.copy(out=target[:, vector_runs:], in_=source[:, vector_runs:])
             return grouped
 
         def quantise(grouped):
@@ -140,29 +143,27 @@ def tile_selfattention_pb_kernel(tc, x, Wq, bq, Wk, bk, out_0, out_1):
             )
             return codes, scales
 
-        def multiply(codes, scales):
-            q_banks = []
-            for first in range(0, SLICES, 2):
-                q_bank = q_psum.tile([P, 2, 2, O], F32)
-                for s in range(2):
-                    for dj in range(2):
-                        start_col = dj * PAIRS + (first + s) * P
-                        cols = slice(start_col, start_col + P)
-                        nc.tensor.matmul_mx(
-                            out=q_bank[:, s, dj, :],
-                            lhsT=codes[:, cols].bitcast(FP8X4),
-                            lhsT_scale=scales[:, cols],
-                            rhs=w_codes[:, 0:O].bitcast(FP8X4),
-                            rhs_scale=w_scales[:, 0:O],
-                            start=True,
-                            stop=True,
-                        )
-                q_banks.append(q_bank)
-            k_bank = k_psum.tile([O, PAIRS], F32)
+        def multiply_queries(codes, scales):
+            q_bank = q_psum.tile([P, SLICES, 2, O], F32)
+            for s in range(SLICES):
+                for dj in range(2):
+                    cols = slice(dj * PAIRS + s * P, dj * PAIRS + (s + 1) * P)
+                    nc.tensor.matmul_mx(
+                        out=q_bank[:, s, dj, :],
+                        lhsT=codes[:, cols].bitcast(FP8X4),
+                        lhsT_scale=scales[:, cols],
+                        rhs=w_codes[:, 0:O].bitcast(FP8X4),
+                        rhs_scale=w_scales[:, 0:O],
+                        start=True,
+                        stop=True,
+                    )
+            return q_bank
+
+        def multiply_keys(codes, scales, k_group):
             for dj in range(2):
                 cols = slice(dj * PAIRS, (dj + 1) * PAIRS)
                 nc.tensor.matmul_mx(
-                    out=k_bank[:],
+                    out=k_group,
                     lhsT=w_codes[:, O : 2 * O].bitcast(FP8X4),
                     lhsT_scale=w_scales[:, O : 2 * O],
                     rhs=codes[:, cols].bitcast(FP8X4),
@@ -170,49 +171,58 @@ def tile_selfattention_pb_kernel(tc, x, Wq, bq, Wk, bk, out_0, out_1):
                     start=(dj == 0),
                     stop=(dj == 1),
                 )
-            return q_banks, k_bank
+
+        def finish_queries(c, q_bank):
+            q_sb = work.tile([P, SLICES, 2 * O], F32)
+            nc.vector.tensor_tensor(
+                out=q_sb[:].rearrange("p s (dj o) -> p (s dj) o", dj=2),
+                in0=q_bank[:].rearrange("p s dj o -> p (s dj) o"),
+                in1=bq_rows[:].unsqueeze(1).to_broadcast([P, 2 * SLICES, O]),
+                op=ADD,
+            )
+            nc.sync.dma_start(out=q_pairs[:, c * SLICES : (c + 1) * SLICES, :], in_=q_sb[:])
+
+        def image_rows(k_bank):
+            return k_bank[:].rearrange("o g (m di n) -> o di (g m) n", di=2, n=POOLED_SIDE)
 
         def lower_rows(k_bank):
-            image_rows = k_bank[:].rearrange("o (m di n) -> o di m n", di=2, n=POOLED_SIDE)
-            lower = work.tile([O, POOLED_ROWS, POOLED_SIDE], F32)
+            lower = work.tile([O, KEY_CHUNKS * POOLED_ROWS, POOLED_SIDE], F32)
             nc.scalar.activation(
-                out=lower[:], in_=image_rows[:, 1], func=IDENTITY, bias=bk_column[:], scale=0.25
+                out=lower[:], in_=image_rows(k_bank)[:, 1], func=IDENTITY, bias=bk_column[:], scale=0.25
             )
             return lower
 
-        def finish(c, q_banks, k_bank, lower):
-            q_sb = work.tile([P, SLICES, 2 * O], F32)
-            for b, q_bank in enumerate(q_banks):
-                nc.vector.tensor_tensor(
-                    out=q_sb[:, 2 * b : 2 * b + 2, :].rearrange("p s (dj o) -> p (s dj) o", dj=2),
-                    in0=q_bank[:].rearrange("p s dj o -> p (s dj) o"),
-                    in1=bq_rows[:].unsqueeze(1).to_broadcast([P, 4, O]),
-                    op=ADD,
-                )
-            nc.sync.dma_start(out=q_pairs[:, c * SLICES : (c + 1) * SLICES, :], in_=q_sb[:])
-
-            image_rows = k_bank[:].rearrange("o (m di n) -> o di m n", di=2, n=POOLED_SIDE)
-            k_sb = work.tile([O, POOLED_ROWS, POOLED_SIDE], F32)
+        def finish_keys(first_chunk, k_bank, lower):
+            k_sb = work.tile([O, KEY_CHUNKS * POOLED_ROWS, POOLED_SIDE], F32)
             nc.vector.scalar_tensor_tensor(
-                out=k_sb[:], in0=image_rows[:, 0], scalar=0.25, in1=lower[:], op0=MULT, op1=ADD
+                out=k_sb[:], in0=image_rows(k_bank)[:, 0], scalar=0.25, in1=lower[:], op0=MULT, op1=ADD
             )
             nc.sync.dma_start(
-                out=k_pool[:, c * POOLED : (c + 1) * POOLED],
+                out=k_pool[:, first_chunk * POOLED : (first_chunk + KEY_CHUNKS) * POOLED],
                 in_=k_sb[:].rearrange("o m n -> o (m n)"),
             )
 
         grouped = regroup(0)
-        w_codes, w_scales = quantise_weights(nc, const, setup_psum, w_rows)
+        w_codes, w_scales = quantise_weights(nc, const, setup_psum, w_rows, identity)
         bq_rows, bk_column = spread_biases(nc, const, setup_psum, row0, ones)
-        earlier = None
+        k_bank = None
         for c in range(N_CHUNKS):
             codes, scales = quantise(grouped)
-            q_banks, k_bank = multiply(codes, scales)
-            if earlier is not None:
-                lower = lower_rows(earlier[1])
+            earlier_q_bank = q_bank if c > 0 else None
+            q_bank = multiply_queries(codes, scales)
+            place = c % KEY_CHUNKS
+            if place == 0:
+                full_k_bank = k_bank
+                k_bank = k_psum.tile([O, KEY_CHUNKS, PAIRS], F32)
+            multiply_keys(codes, scales, k_bank[:, place, :])
+            keys_leave = place == KEY_CHUNKS - 1 and full_k_bank is not None
+            if keys_leave:
+                lower = lower_rows(full_k_bank)
             if c + 1 < N_CHUNKS:
                 grouped = regroup(c + 1)
-            if earlier is not None:
-                finish(c - 1, earlier[0], earlier[1], lower)
-            earlier = (q_banks, k_bank)
-        finish(N_CHUNKS - 1, earlier[0], earlier[1], lower_rows(earlier[1]))
+            if earlier_q_bank is not None:
+                finish_queries(c - 1, earlier_q_bank)
+            if keys_leave:
+                finish_keys(c + 1 - 2 * KEY_CHUNKS, full_k_bank, lower)
+        finish_queries(N_CHUNKS - 1, q_bank)
+        finish_keys(N_CHUNKS - KEY_CHUNKS, k_bank, lower_rows(k_bank))

@@ -30,7 +30,8 @@ POOLED_SIDE = SIDE // 2
 POOLED = POOLED_ROWS * POOLED_SIDE
 KEY_CHUNKS = BANK // PAIRS
 
-VECTOR_PAIRS = PAIRS * 5 // 16
+VECTOR_PAIRS = PAIRS * 3 // 16
+GPSIMD_PAIRS = PAIRS * 3 // 16
 
 FLOPS = 2 * 2 * O * C * PIXELS
 
@@ -38,7 +39,7 @@ assert SIDE % CHUNK_ROWS == 0 and CHUNK_ROWS % 2 == 0
 assert PAIRS in (256, 512)
 assert 2 * SLICES * O <= BANK
 assert N_CHUNKS % KEY_CHUNKS == 0
-assert VECTOR_PAIRS % 4 == 0
+assert VECTOR_PAIRS % 4 == 0 and GPSIMD_PAIRS % 4 == 0
 
 
 def load_weights(nc, const, Wq, Wk):
@@ -129,8 +130,18 @@ def tile_selfattention_pb_kernel(tc, x, Wq, bq, Wk, bk, out_0, out_1):
             target = grouped[:].rearrange("p dj (run pair) t -> p run t pair dj", pair=2)
             source = raws[c][:].rearrange("p t (run pair dj) -> p run t pair dj", pair=2, dj=2)
             vector_runs = VECTOR_PAIRS // 2
+            scalar_runs = (VECTOR_PAIRS + GPSIMD_PAIRS) // 2
             nc.vector.tensor_copy(out=target[:, :vector_runs], in_=source[:, :vector_runs])
-            nc.scalar.copy(out=target[:, vector_runs:], in_=source[:, vector_runs:])
+            nc.scalar.copy(out=target[:, scalar_runs:], in_=source[:, scalar_runs:])
+            gpsimd_pairs = slice(VECTOR_PAIRS, VECTOR_PAIRS + GPSIMD_PAIRS)
+            nc.gpsimd.tensor_scalar(
+                out=grouped[:].rearrange("p dj pair t -> p pair dj t")[:, gpsimd_pairs],
+                in0=raws[c][:].rearrange("p t (pair dj) -> p pair dj t", dj=2)[:, gpsimd_pairs],
+                scalar1=1.0,
+                scalar2=0.0,
+                op0=MULT,
+                op1=ADD,
+            )
             return grouped
 
         def quantise(grouped):

@@ -19,27 +19,19 @@ O = 128
 SIDE = 64
 PIXELS = SIDE * SIDE
 BANK = 512
-
-CHUNK_ROWS = 8
-CHUNK = CHUNK_ROWS * SIDE
-N_CHUNKS = SIDE // CHUNK_ROWS
-PAIRS = CHUNK // 2
-SLICES = PAIRS // P
-POOLED_ROWS = CHUNK_ROWS // 2
 POOLED_SIDE = SIDE // 2
-POOLED = POOLED_ROWS * POOLED_SIDE
-KEY_CHUNKS = BANK // PAIRS
 
-VECTOR_PAIRS = PAIRS * 3 // 16
-GPSIMD_PAIRS = PAIRS * 3 // 16
+CHUNK_ROWS = (8, 8, 8, 8, 8, 8, 8, 8)
+N_CHUNKS = len(CHUNK_ROWS)
+FIRST_ROW = tuple(sum(CHUNK_ROWS[:c]) for c in range(N_CHUNKS))
+BANK_ROWS = 2 * BANK // SIDE
+V_SHARE = (2,) * 8
+G_SHARE = (4,) * 8
+KEY_LAG = 2
 
 FLOPS = 2 * 2 * O * C * PIXELS
 
-assert SIDE % CHUNK_ROWS == 0 and CHUNK_ROWS % 2 == 0
-assert PAIRS in (256, 512)
-assert 2 * SLICES * O <= BANK
-assert N_CHUNKS % KEY_CHUNKS == 0
-assert VECTOR_PAIRS % 4 == 0 and GPSIMD_PAIRS % 4 == 0
+assert sum(CHUNK_ROWS) == SIDE
 
 
 def load_weights(nc, const, Wq, Wk):
@@ -111,9 +103,13 @@ def tile_selfattention_pb_kernel(tc, x, Wq, bq, Wk, bk, out_0, out_1):
         k_psum = ctx.enter_context(tc.psum_pool(name="k_psum", bufs=2))
         ctx.enter_context(tc.manual_schedule())
 
+        def pixels(c):
+            return CHUNK_ROWS[c] * SIDE
+
         def load_chunk(c):
-            raw = raw_pool.tile([P, PACK, CHUNK], BF16)
-            nc.sync.dma_start(out=raw[:], in_=x_rows[:, :, c * CHUNK : (c + 1) * CHUNK])
+            raw = raw_pool.tile([P, PACK, pixels(c)], BF16)
+            first = FIRST_ROW[c] * SIDE
+            nc.sync.dma_start(out=raw[:], in_=x_rows[:, :, first : first + pixels(c)])
             return raw
 
         identity = const.tile([P, P], F32)
@@ -126,27 +122,32 @@ def tile_selfattention_pb_kernel(tc, x, Wq, bq, Wk, bk, out_0, out_1):
             raws.append(load_chunk(c))
 
         def regroup(c):
-            grouped = work.tile([P, 2, PAIRS, PACK], BF16, align_bytes=64)
+            pairs = pixels(c) // 2
+            v_pairs = pairs * V_SHARE[c] // 16
+            g_pairs = pairs * G_SHARE[c] // 16
+            grouped = work.tile([P, 2, pairs, PACK], BF16, align_bytes=64)
             target = grouped[:].rearrange("p dj (run pair) t -> p run t pair dj", pair=2)
             source = raws[c][:].rearrange("p t (run pair dj) -> p run t pair dj", pair=2, dj=2)
-            vector_runs = VECTOR_PAIRS // 2
-            scalar_runs = (VECTOR_PAIRS + GPSIMD_PAIRS) // 2
-            nc.vector.tensor_copy(out=target[:, :vector_runs], in_=source[:, :vector_runs])
+            vector_runs = v_pairs // 2
+            scalar_runs = (v_pairs + g_pairs) // 2
+            if v_pairs:
+                nc.vector.tensor_copy(out=target[:, :vector_runs], in_=source[:, :vector_runs])
             nc.scalar.copy(out=target[:, scalar_runs:], in_=source[:, scalar_runs:])
-            gpsimd_pairs = slice(VECTOR_PAIRS, VECTOR_PAIRS + GPSIMD_PAIRS)
-            nc.gpsimd.tensor_scalar(
-                out=grouped[:].rearrange("p dj pair t -> p pair dj t")[:, gpsimd_pairs],
-                in0=raws[c][:].rearrange("p t (pair dj) -> p pair dj t", dj=2)[:, gpsimd_pairs],
-                scalar1=1.0,
-                scalar2=0.0,
-                op0=MULT,
-                op1=ADD,
-            )
+            if g_pairs:
+                gpsimd_pairs = slice(v_pairs, v_pairs + g_pairs)
+                nc.gpsimd.tensor_scalar(
+                    out=grouped[:].rearrange("p dj pair t -> p pair dj t")[:, gpsimd_pairs],
+                    in0=raws[c][:].rearrange("p t (pair dj) -> p pair dj t", dj=2)[:, gpsimd_pairs],
+                    scalar1=1.0,
+                    scalar2=0.0,
+                    op0=MULT,
+                    op1=ADD,
+                )
             return grouped
 
-        def quantise(grouped):
-            codes = work.tile([P, CHUNK], U32, align_bytes=64)
-            scales = work.tile([P, CHUNK], U8, align_bytes=64)
+        def quantise(c, grouped):
+            codes = work.tile([P, pixels(c)], U32, align_bytes=64)
+            scales = work.tile([P, pixels(c)], U8, align_bytes=64)
             nc.vector.quantize_mx(
                 out=codes[:].bitcast(FP8X4),
                 scales=scales[:],
@@ -154,11 +155,13 @@ def tile_selfattention_pb_kernel(tc, x, Wq, bq, Wk, bk, out_0, out_1):
             )
             return codes, scales
 
-        def multiply_queries(codes, scales):
-            q_bank = q_psum.tile([P, SLICES, 2, O], F32)
-            for s in range(SLICES):
+        def multiply_queries(c, codes, scales):
+            pairs = pixels(c) // 2
+            slices = pairs // P
+            q_bank = q_psum.tile([P, slices, 2, O], F32)
+            for s in range(slices):
                 for dj in range(2):
-                    cols = slice(dj * PAIRS + s * P, dj * PAIRS + (s + 1) * P)
+                    cols = slice(dj * pairs + s * P, dj * pairs + (s + 1) * P)
                     nc.tensor.matmul_mx(
                         out=q_bank[:, s, dj, :],
                         lhsT=codes[:, cols].bitcast(FP8X4),
@@ -170,9 +173,10 @@ def tile_selfattention_pb_kernel(tc, x, Wq, bq, Wk, bk, out_0, out_1):
                     )
             return q_bank
 
-        def multiply_keys(codes, scales, k_group):
+        def multiply_keys(c, codes, scales, k_group):
+            pairs = pixels(c) // 2
             for dj in range(2):
-                cols = slice(dj * PAIRS, (dj + 1) * PAIRS)
+                cols = slice(dj * pairs, (dj + 1) * pairs)
                 nc.tensor.matmul_mx(
                     out=k_group,
                     lhsT=w_codes[:, O : 2 * O].bitcast(FP8X4),
@@ -184,32 +188,34 @@ def tile_selfattention_pb_kernel(tc, x, Wq, bq, Wk, bk, out_0, out_1):
                 )
 
         def finish_queries(c, q_bank):
-            q_sb = work.tile([P, SLICES, 2 * O], F32)
+            slices = pixels(c) // 2 // P
+            first = FIRST_ROW[c] * SIDE // 2 // P
+            q_sb = work.tile([P, slices, 2 * O], F32)
             nc.vector.tensor_tensor(
                 out=q_sb[:].rearrange("p s (dj o) -> p (s dj) o", dj=2),
                 in0=q_bank[:].rearrange("p s dj o -> p (s dj) o"),
-                in1=bq_rows[:].unsqueeze(1).to_broadcast([P, 2 * SLICES, O]),
+                in1=bq_rows[:].unsqueeze(1).to_broadcast([P, 2 * slices, O]),
                 op=ADD,
             )
-            nc.sync.dma_start(out=q_pairs[:, c * SLICES : (c + 1) * SLICES, :], in_=q_sb[:])
+            nc.sync.dma_start(out=q_pairs[:, first : first + slices, :], in_=q_sb[:])
 
         def image_rows(k_bank):
-            return k_bank[:].rearrange("o g (m di n) -> o di (g m) n", di=2, n=POOLED_SIDE)
+            return k_bank[:].rearrange("o (m di n) -> o di m n", di=2, n=POOLED_SIDE)
 
         def lower_rows(k_bank):
-            lower = work.tile([O, KEY_CHUNKS * POOLED_ROWS, POOLED_SIDE], F32)
+            lower = work.tile([O, BANK_ROWS // 2, POOLED_SIDE], F32)
             nc.scalar.activation(
                 out=lower[:], in_=image_rows(k_bank)[:, 1], func=IDENTITY, bias=bk_column[:], scale=0.25
             )
             return lower
 
-        def finish_keys(first_chunk, k_bank, lower):
-            k_sb = work.tile([O, KEY_CHUNKS * POOLED_ROWS, POOLED_SIDE], F32)
+        def finish_keys(b, k_bank, lower):
+            k_sb = work.tile([O, BANK_ROWS // 2, POOLED_SIDE], F32)
             nc.vector.scalar_tensor_tensor(
                 out=k_sb[:], in0=image_rows(k_bank)[:, 0], scalar=0.25, in1=lower[:], op0=MULT, op1=ADD
             )
             nc.sync.dma_start(
-                out=k_pool[:, first_chunk * POOLED : (first_chunk + KEY_CHUNKS) * POOLED],
+                out=k_pool[:, b * BANK // 2 : (b + 1) * BANK // 2],
                 in_=k_sb[:].rearrange("o m n -> o (m n)"),
             )
 
@@ -217,23 +223,28 @@ def tile_selfattention_pb_kernel(tc, x, Wq, bq, Wk, bk, out_0, out_1):
         w_codes, w_scales = quantise_weights(nc, const, setup_psum, w_rows, identity)
         bq_rows, bk_column = spread_biases(nc, const, setup_psum, row0, ones)
         k_bank = None
+        full = []
         for c in range(N_CHUNKS):
-            codes, scales = quantise(grouped)
+            codes, scales = quantise(c, grouped)
             earlier_q_bank = q_bank if c > 0 else None
-            q_bank = multiply_queries(codes, scales)
-            place = c % KEY_CHUNKS
+            q_bank = multiply_queries(c, codes, scales)
+            place = FIRST_ROW[c] % BANK_ROWS
             if place == 0:
-                full_k_bank = k_bank
-                k_bank = k_psum.tile([O, KEY_CHUNKS, PAIRS], F32)
-            multiply_keys(codes, scales, k_bank[:, place, :])
-            keys_leave = place == KEY_CHUNKS - 1 and full_k_bank is not None
+                k_bank = k_psum.tile([O, BANK], F32)
+            k_cols = slice(place * SIDE // 2, (place + CHUNK_ROWS[c]) * SIDE // 2)
+            multiply_keys(c, codes, scales, k_bank[:, k_cols])
+            if (place + CHUNK_ROWS[c]) == BANK_ROWS:
+                full.append((FIRST_ROW[c] // BANK_ROWS, k_bank, c))
+            keys_leave = len(full) > 0 and full[0][2] <= c - KEY_LAG
             if keys_leave:
-                lower = lower_rows(full_k_bank)
+                lower = lower_rows(full[0][1])
             if c + 1 < N_CHUNKS:
                 grouped = regroup(c + 1)
             if earlier_q_bank is not None:
                 finish_queries(c - 1, earlier_q_bank)
             if keys_leave:
-                finish_keys(c + 1 - 2 * KEY_CHUNKS, full_k_bank, lower)
+                finish_keys(full[0][0], full[0][1], lower)
+                full = full[1:]
         finish_queries(N_CHUNKS - 1, q_bank)
-        finish_keys(N_CHUNKS - KEY_CHUNKS, k_bank, lower_rows(k_bank))
+        for b, bank, last in full:
+            finish_keys(b, bank, lower_rows(bank))

@@ -27,6 +27,7 @@ FIRST_ROW = tuple(sum(CHUNK_ROWS[:c]) for c in range(N_CHUNKS))
 BANK_ROWS = 2 * BANK // SIDE
 V_SHARE = (2,) * 8
 G_SHARE = (4,) * 8
+RUN_PAIRS = 4
 KEY_LAG = 2
 
 FLOPS = 2 * 2 * O * C * PIXELS
@@ -126,10 +127,10 @@ def tile_selfattention_pb_kernel(tc, x, Wq, bq, Wk, bk, out_0, out_1):
             v_pairs = pairs * V_SHARE[c] // 16
             g_pairs = pairs * G_SHARE[c] // 16
             grouped = work.tile([P, 2, pairs, PACK], BF16, align_bytes=64)
-            target = grouped[:].rearrange("p dj (run pair) t -> p run t pair dj", pair=2)
-            source = raws[c][:].rearrange("p t (run pair dj) -> p run t pair dj", pair=2, dj=2)
-            vector_runs = v_pairs // 2
-            scalar_runs = (v_pairs + g_pairs) // 2
+            target = grouped[:].rearrange("p dj (run pair) t -> p run t pair dj", pair=RUN_PAIRS)
+            source = raws[c][:].rearrange("p t (run pair dj) -> p run t pair dj", pair=RUN_PAIRS, dj=2)
+            vector_runs = v_pairs // RUN_PAIRS
+            scalar_runs = (v_pairs + g_pairs) // RUN_PAIRS
             if v_pairs:
                 nc.vector.tensor_copy(out=target[:, :vector_runs], in_=source[:, :vector_runs])
             nc.scalar.copy(out=target[:, scalar_runs:], in_=source[:, scalar_runs:])

@@ -99,6 +99,8 @@ def tile_selfattention_pb_kernel(tc, x, Wq, bq, Wk, bk, out_0, out_1):
         const = ctx.enter_context(tc.tile_pool(name="const", bufs=1))
         raw_pool = ctx.enter_context(tc.tile_pool(name="raw", bufs=N_CHUNKS))
         work = ctx.enter_context(tc.tile_pool(name="work", bufs=3))
+        q_out = ctx.enter_context(tc.tile_pool(name="q_out", bufs=N_CHUNKS))
+        k_out = ctx.enter_context(tc.tile_pool(name="k_out", bufs=SIDE // BANK_ROWS))
         setup_psum = ctx.enter_context(tc.psum_pool(name="setup_psum", bufs=1))
         q_psum = ctx.enter_context(tc.psum_pool(name="q_psum", bufs=4))
         k_psum = ctx.enter_context(tc.psum_pool(name="k_psum", bufs=2))
@@ -191,7 +193,7 @@ def tile_selfattention_pb_kernel(tc, x, Wq, bq, Wk, bk, out_0, out_1):
         def finish_queries(c, q_bank):
             slices = pixels(c) // 2 // P
             first = FIRST_ROW[c] * SIDE // 2 // P
-            q_sb = work.tile([P, slices, 2 * O], F32)
+            q_sb = q_out.tile([P, slices, 2 * O], F32)
             nc.vector.tensor_tensor(
                 out=q_sb[:].rearrange("p s (dj o) -> p (s dj) o", dj=2),
                 in0=q_bank[:].rearrange("p s dj o -> p (s dj) o"),
@@ -211,7 +213,7 @@ def tile_selfattention_pb_kernel(tc, x, Wq, bq, Wk, bk, out_0, out_1):
             return lower
 
         def finish_keys(b, k_bank, lower):
-            k_sb = work.tile([O, BANK_ROWS // 2, POOLED_SIDE], F32)
+            k_sb = k_out.tile([O, BANK_ROWS // 2, POOLED_SIDE], F32)
             nc.vector.scalar_tensor_tensor(
                 out=k_sb[:], in0=image_rows(k_bank)[:, 0], scalar=0.25, in1=lower[:], op0=MULT, op1=ADD
             )

@@ -25,8 +25,8 @@ CHUNK_ROWS = (8, 8, 8, 8, 8, 8, 8, 8)
 N_CHUNKS = len(CHUNK_ROWS)
 FIRST_ROW = tuple(sum(CHUNK_ROWS[:c]) for c in range(N_CHUNKS))
 BANK_ROWS = 2 * BANK // SIDE
-V_SHARE = (2,) * 8
-G_SHARE = (4,) * 8
+V_SHARE = (10, 2, 2, 2, 2, 2, 2, 2)
+G_SHARE = (2, 4, 4, 4, 4, 4, 4, 4)
 RUN_PAIRS = 4
 KEY_LAG = 2
 
@@ -54,13 +54,16 @@ def load_biases(nc, const, bq, bk):
     return row0, ones
 
 
-def quantise_weights(nc, const, setup_psum, rows, identity):
+def flip_weights(nc, setup_psum, rows, identity):
     flipped = setup_psum.tile([P, 2, 2, O], F32)
     for i, w_rows in enumerate(rows):
         words = w_rows[:].bitcast(F32).rearrange("o (p u) -> o u p", u=2)
         for u in range(2):
             nc.tensor.transpose(flipped[:, i, u, :], words[:, u, :], identity[:])
+    return flipped
 
+
+def quantise_weights(nc, const, flipped):
     w_grouped = const.tile([P, 2 * O * PACK], BF16, align_bytes=64)
     nc.vector.tensor_copy(
         out=w_grouped[:].bitcast(F32).rearrange("p (i o u) -> p i o u", i=2, u=2),
@@ -223,12 +226,14 @@ def tile_selfattention_pb_kernel(tc, x, Wq, bq, Wk, bk, out_0, out_1):
             )
 
         grouped = regroup(0)
-        w_codes, w_scales = quantise_weights(nc, const, setup_psum, w_rows, identity)
+        flipped = flip_weights(nc, setup_psum, w_rows, identity)
         bq_rows, bk_column = spread_biases(nc, const, setup_psum, row0, ones)
         k_bank = None
         full = []
         for c in range(N_CHUNKS):
             codes, scales = quantise(c, grouped)
+            if c == 0:
+                w_codes, w_scales = quantise_weights(nc, const, flipped)
             earlier_q_bank = q_bank if c > 0 else None
             q_bank = multiply_queries(c, codes, scales)
             place = FIRST_ROW[c] % BANK_ROWS

from contextlib import ExitStack

import concourse.mybir as mybir
from concourse.masks import make_identity

BF16 = mybir.dt.bfloat16
F32 = mybir.dt.float32
U32 = mybir.dt.uint32
U8 = mybir.dt.uint8
FP8X4 = mybir.dt.float8_e4m3fn_x4
ADD = mybir.AluOpType.add
MULT = mybir.AluOpType.mult
IDENTITY = mybir.ActivationFunctionType.Identity

P = 128
PACK = 4
C = P * PACK
O = 128
SIDE = 64
PIXELS = SIDE * SIDE
BANK = 512
POOLED_SIDE = SIDE // 2

CHUNK_ROWS = (8, 8, 8, 8, 8, 8, 8, 8)
N_CHUNKS = len(CHUNK_ROWS)
FIRST_ROW = tuple(sum(CHUNK_ROWS[:c]) for c in range(N_CHUNKS))
BANK_ROWS = 2 * BANK // SIDE
V_SHARE = (10, 2, 2, 2, 2, 2, 2, 2)
G_SHARE = (2, 4, 4, 4, 4, 4, 4, 4)
RUN_PAIRS = 4
KEY_LAG = 2

FLOPS = 2 * 2 * O * C * PIXELS

assert sum(CHUNK_ROWS) == SIDE


def load_weights(nc, const, Wq, Wk):
    rows = []
    for i, weight in enumerate((Wq, Wk)):
        w_rows = const.tile([O, C], BF16, name="w_rows%d" % i)
        nc.sync.dma_start(out=w_rows[:], in_=weight)
        rows.append(w_rows)
    return rows


def load_biases(nc, const, bq, bk):
    row0 = const.tile([P, 2 * O], BF16)
    nc.vector.memset(row0[:], 0.0)
    nc.sync.dma_start(out=row0[0:1, 0:O], in_=bq.unsqueeze(0))
    nc.sync.dma_start(out=row0[0:1, O : 2 * O], in_=bk.unsqueeze(0))
    ones = const.tile([P, P], BF16)
    nc.vector.memset(ones[:], 1.0)
    return row0, ones


def flip_weights(nc, setup_psum, rows, identity):
    flipped = setup_psum.tile([P, 2, 2, O], F32)
    for i, w_rows in enumerate(rows):
        words = w_rows[:].bitcast(F32).rearrange("o (p u) -> o u p", u=2)
        for u in range(2):
            nc.tensor.transpose(flipped[:, i, u, :], words[:, u, :], identity[:])
    return flipped


def quantise_weights(nc, const, flipped):
    w_grouped = const.tile([P, 2 * O * PACK], BF16, align_bytes=64)
    nc.vector.tensor_copy(
        out=w_grouped[:].bitcast(F32).rearrange("p (i o u) -> p i o u", i=2, u=2),
        in_=flipped[:].rearrange("p i u o -> p i o u"),
    )
    w_codes = const.tile([P, 2 * O], U32, align_bytes=64)
    w_scales = const.tile([P, 2 * O], U8, align_bytes=64)
    nc.vector.quantize_mx(out=w_codes[:].bitcast(FP8X4), scales=w_scales[:], in_=w_grouped[:])
    return w_codes, w_scales


def spread_biases(nc, const, setup_psum, row0, ones):
    spread = setup_psum.tile([P, BANK], F32)
    nc.tensor.matmul(out=spread[:, 0 : 2 * O], lhsT=ones[:], rhs=row0[:], start=True, stop=True)
    nc.tensor.matmul(
        out=spread[:, 2 * O : 2 * O + 32],
        lhsT=row0[:, O : 2 * O],
        rhs=ones[:, 0:32],
        start=True,
        stop=True,
    )
    bq_rows = const.tile([P, O], F32)
    nc.scalar.activation(out=bq_rows[:], in_=spread[:, 0:O], func=IDENTITY)
    bk_column = const.tile([O, 1], F32)
    nc.scalar.activation(out=bk_column[:], in_=spread[:, 2 * O : 2 * O + 1], func=IDENTITY)
    return bq_rows, bk_column


def tile_selfattention_pb_kernel(tc, x, Wq, bq, Wk, bk, out_0, out_1):
    nc = tc.nc
    x_rows = x[0].rearrange("(p t) h w -> p t (h w)", t=PACK)
    q_pairs = out_0[0].rearrange("(s p dj) o -> p s (dj o)", p=P, dj=2)
    k_pool = out_1[0]

    with ExitStack() as ctx:
        const = ctx.enter_context(tc.tile_pool(name="const", bufs=1))
        raw_pool = ctx.enter_context(tc.tile_pool(name="raw", bufs=N_CHUNKS))
        work = ctx.enter_context(tc.tile_pool(name="work", bufs=3))
        q_out = ctx.enter_context(tc.tile_pool(name="q_out", bufs=N_CHUNKS))
        k_out = ctx.enter_context(tc.tile_pool(name="k_out", bufs=SIDE // BANK_ROWS))
        setup_psum = ctx.enter_context(tc.psum_pool(name="setup_psum", bufs=1))
        q_psum = ctx.enter_context(tc.psum_pool(name="q_psum", bufs=4))
        k_psum = ctx.enter_context(tc.psum_pool(name="k_psum", bufs=2))
        ctx.enter_context(tc.manual_schedule())

        def pixels(c):
            return CHUNK_ROWS[c] * SIDE

        def load_chunk(c):
            raw = raw_pool.tile([P, PACK, pixels(c)], BF16)
            first = FIRST_ROW[c] * SIDE
            nc.sync.dma_start(out=raw[:], in_=x_rows[:, :, first : first + pixels(c)])
            return raw

        identity = const.tile([P, P], F32)
        make_identity(nc, identity[:])

        raws = [load_chunk(0)]
        w_rows = load_weights(nc, const, Wq, Wk)
        row0, ones = load_biases(nc, const, bq, bk)
        for c in range(1, N_CHUNKS):
            raws.append(load_chunk(c))

        def regroup(c):
            pairs = pixels(c) // 2
            v_pairs = pairs * V_SHARE[c] // 16
            g_pairs = pairs * G_SHARE[c] // 16
            grouped = work.tile([P, 2, pairs, PACK], BF16, align_bytes=64)
            target = grouped[:].rearrange("p dj (run pair) t -> p run t pair dj", pair=RUN_PAIRS)
            source = raws[c][:].rearrange("p t (run pair dj) -> p run t pair dj", pair=RUN_PAIRS, dj=2)
            vector_runs = v_pairs // RUN_PAIRS
            scalar_runs = (v_pairs + g_pairs) // RUN_PAIRS
            if v_pairs:
                nc.vector.tensor_copy(out=target[:, :vector_runs], in_=source[:, :vector_runs])
            nc.scalar.copy(out=target[:, scalar_runs:], in_=source[:, scalar_runs:])
            if g_pairs:
                gpsimd_pairs = slice(v_pairs, v_pairs + g_pairs)
                nc.gpsimd.tensor_scalar(
                    out=grouped[:].rearrange("p dj pair t -> p pair dj t")[:, gpsimd_pairs],
                    in0=raws[c][:].rearrange("p t (pair dj) -> p pair dj t", dj=2)[:, gpsimd_pairs],
                    scalar1=1.0,
                    scalar2=0.0,
                    op0=MULT,
                    op1=ADD,
                )
            return grouped

        def quantise(c, grouped):
            codes = work.tile([P, pixels(c)], U32, align_bytes=64)
            scales = work.tile([P, pixels(c)], U8, align_bytes=64)
            nc.vector.quantize_mx(
                out=codes[:].bitcast(FP8X4),
                scales=scales[:],
                in_=grouped[:].rearrange("p dj pair t -> p (dj pair t)"),
            )
            return codes, scales

        def multiply_queries(c, codes, scales):
            pairs = pixels(c) // 2
            slices = pairs // P
            q_bank = q_psum.tile([P, slices, 2, O], F32)
            for s in range(slices):
                for dj in range(2):
                    cols = slice(dj * pairs + s * P, dj * pairs + (s + 1) * P)
                    nc.tensor.matmul_mx(
                        out=q_bank[:, s, dj, :],
                        lhsT=codes[:, cols].bitcast(FP8X4),
                        lhsT_scale=scales[:, cols],
                        rhs=w_codes[:, 0:O].bitcast(FP8X4),
                        rhs_scale=w_scales[:, 0:O],
                        start=True,
                        stop=True,
                    )
            return q_bank

        def multiply_keys(c, codes, scales, k_group):
            pairs = pixels(c) // 2
            for dj in range(2):
                cols = slice(dj * pairs, (dj + 1) * pairs)
                nc.tensor.matmul_mx(
                    out=k_group,
                    lhsT=w_codes[:, O : 2 * O].bitcast(FP8X4),
                    lhsT_scale=w_scales[:, O : 2 * O],
                    rhs=codes[:, cols].bitcast(FP8X4),
                    rhs_scale=scales[:, cols],
                    start=(dj == 0),
                    stop=(dj == 1),
                )

        def finish_queries(c, q_bank):
            slices = pixels(c) // 2 // P
            first = FIRST_ROW[c] * SIDE // 2 // P
            q_sb = q_out.tile([P, slices, 2 * O], F32)
            nc.vector.tensor_tensor(
                out=q_sb[:].rearrange("p s (dj o) -> p (s dj) o", dj=2),
                in0=q_bank[:].rearrange("p s dj o -> p (s dj) o"),
                in1=bq_rows[:].unsqueeze(1).to_broadcast([P, 2 * slices, O]),
                op=ADD,
            )
            nc.sync.dma_start(out=q_pairs[:, first : first + slices, :], in_=q_sb[:])

        def image_rows(k_bank):
            return k_bank[:].rearrange("o (m di n) -> o di m n", di=2, n=POOLED_SIDE)

        def lower_rows(k_bank):
            lower = work.tile([O, BANK_ROWS // 2, POOLED_SIDE], F32)
            nc.scalar.activation(
                out=lower[:], in_=image_rows(k_bank)[:, 1], func=IDENTITY, bias=bk_column[:], scale=0.25
            )
            return lower

        def finish_keys(b, k_bank, lower):
            k_sb = k_out.tile([O, BANK_ROWS // 2, POOLED_SIDE], F32)
            nc.vector.scalar_tensor_tensor(
                out=k_sb[:], in0=image_rows(k_bank)[:, 0], scalar=0.25, in1=lower[:], op0=MULT, op1=ADD
            )
            nc.sync.dma_start(
                out=k_pool[:, b * BANK // 2 : (b + 1) * BANK // 2],
                in_=k_sb[:].rearrange("o m n -> o (m n)"),
            )

        grouped = regroup(0)
        flipped = flip_weights(nc, setup_psum, w_rows, identity)
        bq_rows, bk_column = spread_biases(nc, const, setup_psum, row0, ones)
        k_bank = None
        full = []
        for c in range(N_CHUNKS):
            codes, scales = quantise(c, grouped)
            if c == 0:
                w_codes, w_scales = quantise_weights(nc, const, flipped)
            earlier_q_bank = q_bank if c > 0 else None
            q_bank = multiply_queries(c, codes, scales)
            place = FIRST_ROW[c] % BANK_ROWS
            if place == 0:
                k_bank = k_psum.tile([O, BANK], F32)
            k_cols = slice(place * SIDE // 2, (place + CHUNK_ROWS[c]) * SIDE // 2)
            multiply_keys(c, codes, scales, k_bank[:, k_cols])
            if (place + CHUNK_ROWS[c]) == BANK_ROWS:
                full.append((FIRST_ROW[c] // BANK_ROWS, k_bank, c))
            keys_leave = len(full) > 0 and full[0][2] <= c - KEY_LAG
            if keys_leave:
                lower = lower_rows(full[0][1])
            if c + 1 < N_CHUNKS:
                grouped = regroup(c + 1)
            if earlier_q_bank is not None:
                finish_queries(c - 1, earlier_q_bank)
            if keys_leave:
                finish_keys(full[0][0], full[0][1], lower)
                full = full[1:]
        finish_queries(N_CHUNKS - 1, q_bank)
        for b, bank, last in full:
            finish_keys(b, bank, lower_rows(bank))
